import numpy as np
import ml_dtypes


def mxq(x, axis, fmt="e4m3"):
    dtype, down = {"e4m3": (ml_dtypes.float8_e4m3fn, 7), "e5m2": (ml_dtypes.float8_e5m2, 14)}[fmt]
    v = np.moveaxis(np.asarray(x, np.float32).astype(ml_dtypes.bfloat16).astype(np.float64), axis, -1)
    blocks = v.reshape(v.shape[:-1] + (-1, 32))
    amax = np.abs(blocks).max(-1, keepdims=True)
    byte = np.maximum(np.where(amax > 0, np.frexp(amax)[1] - 1 + 127, 0) - down, 1)
    scale = np.exp2(byte - 127.0)
    codes = (blocks / scale).astype(np.float32).astype(dtype).astype(np.float64)
    return np.moveaxis((codes * scale).reshape(v.shape), -1, axis)


WIDE = False


def mx_kscale(k):
    if not WIDE:
        return np.ones(k)
    levels = np.array([10, -10, 5, -5, 0])
    if k % 512:
        return np.exp2(np.random.permutation(np.resize(levels, k // 32))).repeat(32)
    a = np.empty((k // 512, 16))
    for p in range(k // 512):
        a[p, :8] = np.random.permutation(np.resize(levels, 8))
        for g in range(8):
            far = levels[np.abs(levels - a[p, g]) >= 10]
            a[p, g + 8] = far[np.random.randint(len(far))]
    return np.exp2(a.ravel()).repeat(32)


BF16 = ml_dtypes.bfloat16


def bf(x):
    return np.asarray(x, np.float32).astype(BF16)


def f64(x):
    return np.asarray(x).astype(np.float64)


B, T, D, H, DK, ROPE, NOPE, VD, KVR, QR = 1, 8192, 512, 2, 128, 64, 64, 128, 512, 1024
EPS = 1.1920928955078125e-07
HALF = ROPE // 2


def rms_norm(h, w):
    var = np.mean(h * h, axis=-1, keepdims=True)
    return h * (1.0 / np.sqrt(var + EPS)) * w


def rope(v):
    inv_freq = 1.0 / (10000.0 ** (f64(np.arange(0, ROPE, 2)) / ROPE))
    freqs = np.outer(f64(np.arange(v.shape[-2])), inv_freq)
    cos, sin = np.cos(freqs), np.sin(freqs)
    v1, v2 = v[..., :HALF], v[..., HALF:]
    return np.concatenate([v1 * cos - v2 * sin, v1 * sin + v2 * cos], axis=-1)


def setup_inputs():
    s, t = mx_kscale(D), mx_kscale(KVR)
    return {'x': bf(np.random.standard_normal((B, T, D)) * s),
            'wkv_c': bf(np.random.standard_normal((D, KVR)) / np.sqrt(D) / s[:, None]),
            'kv_a_norm_w': bf((1.0 + 0.1 * np.random.standard_normal(KVR)) * t),
            'wkv_b': bf(np.random.standard_normal((KVR, H * (NOPE + VD))) / np.sqrt(KVR) / t[:, None]),
            'k_pe': bf(np.random.standard_normal((B, T, ROPE)))}


def reference(x, wkv_c, kv_a_norm_w, wkv_b, k_pe):
    c = mxq(f64(x), 2, 'e4m3') @ mxq(f64(wkv_c), 0, 'e4m3')
    cn = rms_norm(c, f64(kv_a_norm_w))
    kv = mxq(cn, 2, 'e4m3') @ mxq(f64(wkv_b), 0, 'e4m3')
    kv = kv.reshape(B, T, H, NOPE + VD).transpose(0, 2, 1, 3)
    k_nope, v = kv[..., :NOPE], kv[..., NOPE:]
    k_rot = rope(f64(k_pe)[:, None])
    k_rot = np.broadcast_to(k_rot, (B, H, T, ROPE))
    ks = np.concatenate([k_nope, k_rot], axis=-1)
    return ks, np.ascontiguousarray(v)

@@ -1,0 +1,320 @@
+from contextlib import ExitStack
+
+import concourse.mybir as mybir
+from concourse.masks import make_identity
+
+F32 = mybir.dt.float32
+BF16 = mybir.dt.bfloat16
+U32 = mybir.dt.uint32
+U8 = mybir.dt.uint8
+I32 = mybir.dt.int32
+FP8X4 = mybir.dt.float8_e4m3fn_x4
+ALU = mybir.AluOpType
+ACT = mybir.ActivationFunctionType
+
+P = 128
+PACK = 4
+T = 8192
+D = 512
+KVR = 512
+H = 2
+NOPE = 64
+VD = 128
+ROPE = 64
+HALF = ROPE // 2
+EPS = 1.1920928955078125e-07
+PI = 3.141592653589793
+TPP = T // P
+CH = 8
+NCH = TPP // CH
+NPAIR = TPP // 2
+PPC = CH // 2
+PW = 2 * P
+RG = 4
+X_BUFS = 4
+
+FLOPS = 2 * T * D * KVR + 2 * T * KVR * H * (NOPE + VD)
+
+
+def tile_deepseekmultiheadattention_pb_t_kernel(tc, x, wkv_c, kv_a_norm_w, wkv_b, k_pe, out_0, out_1):
+    nc = tc.nc
+    x_view = x.flatten_outer_dims().rearrange("(p i) k -> p i k", i=TPP)
+    kpe_view = k_pe.flatten_outer_dims().rearrange("(p i) d -> p i d", i=TPP)
+    ks_view = out_0.rearrange("o h (p i) d -> p (o h) i d", i=TPP)
+    v_view = out_1.rearrange("o h (p i) d -> p (o h) i d", i=TPP)
+
+    with ExitStack() as ctx:
+        const = ctx.enter_context(tc.tile_pool(name="const", bufs=1))
+        xin = ctx.enter_context(tc.tile_pool(name="xin", bufs=X_BUFS))
+        work = ctx.enter_context(tc.tile_pool(name="work", bufs=3))
+        small = ctx.enter_context(tc.tile_pool(name="small", bufs=4))
+        vout = ctx.enter_context(tc.tile_pool(name="vout", bufs=3))
+        turn = ctx.enter_context(tc.tile_pool(name="turn", bufs=2))
+        psum = ctx.enter_context(tc.psum_pool(name="psum", bufs=1))
+        ctx.enter_context(tc.manual_schedule())
+
+        x_chunks = {}
+
+        def load_x(chunk, pieces):
+            xc = xin.tile([P, CH, D], BF16, name="xc")
+            lo = 0
+            for count in pieces:
+                nc.sync.dma_start(out=xc[:, lo:lo + count, :],
+                                  in_=x_view[:, chunk * CH + lo:chunk * CH + lo + count, :])
+                lo += count
+            x_chunks[chunk] = xc
+
+        wc_raw = const.tile([P, PACK, KVR], BF16, name="wc_raw")
+        wb_raw = const.tile([P, PACK, H * (NOPE + VD)], BF16, name="wb_raw")
+        gain_raw = const.tile([P, KVR], BF16, name="gain_raw")
+        gain = const.tile([P, KVR], BF16, name="gain")
+        kpe = const.tile([P, TPP, ROPE], BF16, name="kpe")
+
+        load_x(0, [2, CH - 2])
+        nc.scalar.dma_start(out=wc_raw[:], in_=wkv_c.rearrange("(p t) f -> p t f", t=PACK))
+        nc.scalar.dma_start(out=gain_raw[:], in_=kv_a_norm_w.partition_broadcast(P))
+        nc.sync.dma_start(out=wb_raw[:], in_=wkv_b.rearrange("(p t) w -> p t w", t=PACK))
+        load_x(1, [CH])
+        nc.sync.dma_start(out=kpe[:], in_=kpe_view)
+        for chunk in range(2, X_BUFS):
+            load_x(chunk, [CH])
+
+        NPOS = NCH + CH
+        pos = const.tile([P, NPOS], F32, name="pos")
+        nc.gpsimd.iota(pos[:, 0:NCH], pattern=[[CH, NCH]], base=0, channel_multiplier=TPP,
+                       allow_small_or_imprecise_dtypes=True)
+        nc.gpsimd.iota(pos[:, NCH:NPOS], pattern=[[1, CH]], base=0, channel_multiplier=0,
+                       allow_small_or_imprecise_dtypes=True)
+        ident_f = const.tile([P, P], F32, name="ident_f")
+        make_identity(nc, ident_f[:])
+        ident_b = const.tile([P, P], BF16, name="ident_b")
+        make_identity(nc, ident_b[:])
+        eps_t = const.tile([P, 1], F32, name="eps_t")
+        nc.vector.memset(eps_t[:], EPS)
+        one_t = const.tile([P, 1], F32, name="one_t")
+        nc.vector.memset(one_t[:], 1.0)
+
+        freq = const.tile([P, HALF], F32, name="freq")
+        turns = const.tile([P, NPOS, HALF], F32, name="turns")
+        whole = const.tile([P, NPOS, HALF], I32, name="whole")
+        sin_t = const.tile([P, NPOS, HALF], F32, name="sin_t")
+        cos_t = const.tile([P, NPOS, HALF], F32, name="cos_t")
+        unused = const.tile([P, 1], F32, name="unused")
+
+        def reduce_angles():
+            for j in range(HALF):
+                turns_a_position = 10000.0 ** (-j / float(HALF)) / (2.0 * PI)
+                if j < HALF // 2:
+                    nc.vector.tensor_scalar(out=freq[:, j:j + 1], in0=one_t[:], scalar1=turns_a_position, scalar2=None,
+                                            op0=ALU.mult)
+                else:
+                    nc.scalar.mul(out=freq[:, j:j + 1], in_=one_t[:], mul=turns_a_position)
+            nc.vector.tensor_tensor(out=turns[:], in0=pos[:].unsqueeze(2).to_broadcast([P, NPOS, HALF]),
+                                    in1=freq[:].unsqueeze(1).to_broadcast([P, NPOS, HALF]), op=ALU.mult)
+            nc.vector.tensor_copy(out=whole[:], in_=turns[:])
+            nc.vector.tensor_tensor(out=turns[:], in0=turns[:], in1=whole[:], op=ALU.subtract)
+
+        def make_tables():
+            nc.scalar.activation(out=sin_t[:], in_=turns[:], func=ACT.Sin, scale=2.0 * PI)
+            nc.scalar.activation(out=cos_t[:], in_=turns[:], func=ACT.Sin, scale=PI)
+            nc.scalar.activation(out=unused[:], in_=one_t[:], func=ACT.Abs_reciprocal_sqrt)
+            nc.gpsimd.tensor_tensor(out=cos_t[:], in0=cos_t[:], in1=cos_t[:], op=ALU.mult)
+            nc.gpsimd.tensor_scalar(out=cos_t[:], in0=cos_t[:], scalar1=-2.0, scalar2=1.0, op0=ALU.mult, op1=ALU.add)
+
+        wc_words = const.tile([P, KVR], U32, name="wc_words", align_bytes=64)
+        wc_scales = const.tile([P, KVR], U8, name="wc_scales", align_bytes=64)
+        wv_words = const.tile([P, H * VD], U32, name="wv_words", align_bytes=64)
+        wv_scales = const.tile([P, H * VD], U8, name="wv_scales", align_bytes=64)
+        wk_words = const.tile([P, H * NOPE], U32, name="wk_words", align_bytes=64)
+        wk_scales = const.tile([P, H * NOPE], U8, name="wk_scales", align_bytes=64)
+
+        def quantise_wkv_c():
+            wc_grouped = const.tile([P, KVR * PACK], BF16, name="wc_grouped", align_bytes=64)
+            nc.vector.tensor_copy(out=wc_grouped[:].rearrange("p (t m j) -> p t m j", t=PACK, j=PACK),
+                                  in_=wc_raw[:].rearrange("p j (m t) -> p t m j", t=PACK))
+            nc.vector.quantize_mx(out=wc_words[:].bitcast(FP8X4), scales=wc_scales[:], in_=wc_grouped[:])
+            nc.vector.tensor_copy(out=gain[:].rearrange("p (t m) -> p t m", t=PACK),
+                                  in_=gain_raw[:].rearrange("p (m t) -> p t m", t=PACK))
+
+        def quantise_wkv_b():
+            by_head = wb_raw[:].rearrange("p t (h d) -> p t h d", h=H)
+            wv_grouped = const.tile([P, H, VD, PACK], BF16, name="wv_grouped", align_bytes=64)
+            wk_grouped = const.tile([P, H, NOPE, PACK], BF16, name="wk_grouped", align_bytes=64)
+            nc.vector.tensor_copy(out=wv_grouped[:], in_=by_head[:, :, :, NOPE:NOPE + VD].rearrange("p t h d -> p h d t"))
+            nc.vector.tensor_copy(out=wk_grouped[:], in_=by_head[:, :, :, 0:NOPE].rearrange("p t h d -> p h d t"))
+            nc.vector.quantize_mx(out=wv_words[:].bitcast(FP8X4), scales=wv_scales[:],
+                                  in_=wv_grouped[:].rearrange("p h d t -> p (h d t)"))
+            nc.vector.quantize_mx(out=wk_words[:].bitcast(FP8X4), scales=wk_scales[:],
+                                  in_=wk_grouped[:].rearrange("p h d t -> p (h d t)"))
+
+        ks_chunks = {}
+        for chunk in range(NCH):
+            ks_chunks[chunk] = const.tile([P, H, CH, NOPE + ROPE], F32, name="ks%d" % chunk)
+
+        def rotate(out_lo, out_hi, src, cos_a, sin_a):
+            by_cos = turn.tile([P, RG, 2, HALF], F32, name="by_cos")
+            by_sin = turn.tile([P, RG, 2, HALF], F32, name="by_sin")
+            nc.gpsimd.tensor_tensor(out=by_cos[:], in0=src, in1=cos_a, op=ALU.mult)
+            nc.gpsimd.tensor_tensor(out=by_sin[:], in0=src, in1=sin_a, op=ALU.mult)
+            nc.gpsimd.tensor_tensor(out=out_lo, in0=by_cos[:, :, 0, :], in1=by_sin[:, :, 1, :], op=ALU.subtract)
+            nc.gpsimd.tensor_tensor(out=out_hi, in0=by_sin[:, :, 0, :], in1=by_cos[:, :, 1, :], op=ALU.add)
+
+        def rotate_keys(g):
+            shape = [P, RG, 2, HALF]
+            chunk = g * RG // CH
+            b = g * RG % CH
+            once = turn.tile([P, RG, 2, HALF], F32, name="once")
+            rotate(once[:, :, 0, :], once[:, :, 1, :],
+                   kpe[:, g * RG:(g + 1) * RG, :].rearrange("p i (s j) -> p i s j", s=2),
+                   cos_t[:, NCH + b:NCH + b + RG, :].unsqueeze(2).to_broadcast(shape),
+                   sin_t[:, NCH + b:NCH + b + RG, :].unsqueeze(2).to_broadcast(shape))
+            rows = ks_chunks[chunk][:, 0, b:b + RG, :]
+            rotate(rows[:, :, NOPE:NOPE + HALF], rows[:, :, NOPE + HALF:NOPE + ROPE], once[:],
+                   cos_t[:, chunk:chunk + 1, :].unsqueeze(2).to_broadcast(shape),
+                   sin_t[:, chunk:chunk + 1, :].unsqueeze(2).to_broadcast(shape))
+
+        live = {}
+
+        def on(n):
+            return 0 <= n < NPAIR
+
+        def grouped(period):
+            if ("grouped", period) not in live:
+                live["grouped", period] = work.tile([P, 2 * PW * PACK], BF16, name="grouped", align_bytes=64)
+            return live["grouped", period]
+
+        def transpose_x(n):
+            xc = x_chunks[n // PPC]
+            xt = psum.tile([P, 2, 2, P], F32, name="xt")
+            for a in range(2):
+                as_f32 = xc[:, 2 * (n % PPC) + a, :].bitcast(F32)
+                for u in range(2):
+                    nc.tensor.transpose(xt[:, a, u, :], as_f32[:, u:2 * P:2], ident_f[:])
+            live["xt", n] = xt
+
+        def copy_x(n):
+            nc.scalar.copy(out=grouped(n)[:, 0:PW * PACK].bitcast(F32).rearrange("p (a r u) -> p a r u", a=2, u=2),
+                           in_=live["xt", n][:].rearrange("p a u r -> p a r u"))
+
+        def quantise(period):
+            lo = 0 if on(period) else PW
+            hi = 2 * PW if on(period - 3) else PW
+            words = work.tile([P, 2 * PW], U32, name="words", align_bytes=64)
+            scales = work.tile([P, 2 * PW], U8, name="scales", align_bytes=64)
+            nc.vector.quantize_mx(out=words[:, lo:hi].bitcast(FP8X4), scales=scales[:, lo:hi],
+                                  in_=grouped(period)[:, PACK * lo:PACK * hi])
+            live["quantised", period] = (words, scales)
+
+        def matmul_1(n):
+            words, scales = live["quantised", n]
+            for a in range(2):
+                c_ps = psum.tile([P, KVR], F32, name="c_ps", bufs=4)
+                nc.tensor.matmul_mx(out=c_ps[:], lhsT=words[:, P * a:P * a + P].bitcast(FP8X4),
+                                    lhsT_scale=scales[:, P * a:P * a + P],
+                                    rhs=wc_words[:].bitcast(FP8X4), rhs_scale=wc_scales[:], start=True, stop=True)
+                live["c", n, a] = c_ps
+
+        def statistics(n):
+            sums = small.tile([P, 2], F32, name="sums")
+            for a in range(2):
+                squares = work.tile([P, KVR], BF16, name="squares")
+                nc.scalar.activation(out=squares[:], in_=live["c", n, a][:], func=ACT.Square, accum_out=sums[:, a:a + 1])
+            rstd = small.tile([P, 2], F32, name="rstd")
+            nc.scalar.activation(out=rstd[:], in_=sums[:], func=ACT.Abs_reciprocal_sqrt, scale=1.0 / KVR, bias=eps_t[:])
+            live["rstd", n] = rstd
+
+        def normalise(n, a):
+            if a == 0:
+                live["cn", n] = work.tile([P, 2, KVR], BF16, name="cn")
+            nc.vector.scalar_tensor_tensor(out=live["cn", n][:, a, :], in0=live["c", n, a][:],
+                                           scalar=live["rstd", n][:, a:a + 1], in1=gain[:], op0=ALU.mult, op1=ALU.mult)
+
+        def transpose_cn(n):
+            cn = live["cn", n]
+            cnt = psum.tile([P, 2, PACK, P], BF16, name="cnt")
+            for a in range(2):
+                for t in range(PACK):
+                    nc.tensor.transpose(cnt[:, a, t, :], cn[:, a, P * t:P * t + P], ident_b[:])
+            live["cnt", n] = cnt
+
+        def copy_cn(n):
+            dst = grouped(n + 3)[:, PW * PACK:2 * PW * PACK].rearrange("p (a r t) -> p a r t", a=2, t=PACK)
+            src = live["cnt", n][:].rearrange("p a t r -> p a r t")
+            if n >= NPAIR - 2:
+                nc.scalar.copy(out=dst, in_=src)
+            else:
+                nc.vector.tensor_copy(out=dst, in_=src)
+
+        def matmul_2(n):
+            words, scales = live["quantised", n + 3]
+            v_ps = psum.tile([P, 2, H * VD], F32, name="v_ps")
+            k_ps = psum.tile([P, 2, H * NOPE], F32, name="k_ps")
+            for a in range(2):
+                lo = PW + P * a
+                nc.tensor.matmul_mx(out=v_ps[:, a, :], lhsT=words[:, lo:lo + P].bitcast(FP8X4),
+                                    lhsT_scale=scales[:, lo:lo + P],
+                                    rhs=wv_words[:].bitcast(FP8X4), rhs_scale=wv_scales[:], start=True, stop=True)
+                nc.tensor.matmul_mx(out=k_ps[:, a, :], lhsT=words[:, lo:lo + P].bitcast(FP8X4),
+                                    lhsT_scale=scales[:, lo:lo + P],
+                                    rhs=wk_words[:].bitcast(FP8X4), rhs_scale=wk_scales[:], start=True, stop=True)
+            live["v", n] = v_ps
+            live["k", n] = k_ps
+
+        v_chunks = {}
+
+        def store(chunk, i0, count):
+            lo = chunk * CH + i0
+            hi = lo + count
+            ks = ks_chunks[chunk]
+            nc.sync.dma_start(out=v_view[:, :, lo:hi, :], in_=v_chunks[chunk][:, :, i0:i0 + count, :])
+            nc.sync.dma_start(out=ks_view[:, 0, lo:hi, :], in_=ks[:, 0, i0:i0 + count, :])
+            nc.sync.dma_start(out=ks_view[:, 1, lo:hi, 0:NOPE], in_=ks[:, 1, i0:i0 + count, 0:NOPE])
+            nc.sync.dma_start(out=ks_view[:, 1, lo:hi, NOPE:NOPE + ROPE], in_=ks[:, 0, i0:i0 + count, NOPE:NOPE + ROPE])
+
+        def copy_kv(n):
+            chunk = n // PPC
+            i0 = 2 * (n % PPC)
+            if n % PPC == 0:
+                v_chunks[chunk] = vout.tile([P, H, CH, VD], F32, name="v_sb")
+            nc.scalar.copy(out=v_chunks[chunk][:, :, i0:i0 + 2, :],
+                           in_=live["v", n][:].rearrange("p a (h d) -> p h a d", h=H))
+            nc.scalar.copy(out=ks_chunks[chunk][:, :, i0:i0 + 2, 0:NOPE],
+                           in_=live["k", n][:].rearrange("p a (h d) -> p h a d", h=H))
+            if chunk == NCH - 1:
+                store(chunk, i0, 2)
+            elif n % PPC == PPC - 1:
+                store(chunk, 0, CH)
+
+        reduce_angles()
+        quantise_wkv_c()
+        for m in range(-1, NPAIR + 4):
+            if on(m - 1):
+                matmul_1(m - 1)
+            if on(m - 4):
+                matmul_2(m - 4)
+            if on(m - 1):
+                statistics(m - 1)
+            if on(m - 4):
+                copy_kv(m - 4)
+            if on(m - 2):
+                normalise(m - 2, 0)
+            if on(m - 3):
+                copy_cn(m - 3)
+            if on(m - 2):
+                normalise(m - 2, 1)
+            if on(m + 1):
+                transpose_x(m + 1)
+                if (m + 1) % PPC == PPC - 1 and (m + 1) // PPC + X_BUFS < NCH:
+                    load_x((m + 1) // PPC + X_BUFS, [CH])
+            if on(m - 2):
+                transpose_cn(m - 2)
+            if on(m + 1):
+                copy_x(m + 1)
+            if on(m) or on(m - 3):
+                quantise(m)
+            if m == -1:
+                make_tables()
+            if m == 1:
+                quantise_wkv_b()
+            if 0 <= m < TPP // RG:
+                rotate_keys(m)

@@ -87,8 +87,6 @@ def tile_deepseekmultiheadattention_pb_t_kernel(tc, x, wkv_c, kv_a_norm_w, wkv_b
                        allow_small_or_imprecise_dtypes=True)
         ident_f = const.tile([P, P], F32, name="ident_f")
         make_identity(nc, ident_f[:])
-        ident_b = const.tile([P, P], BF16, name="ident_b")
-        make_identity(nc, ident_b[:])
         eps_t = const.tile([P, 1], F32, name="eps_t")
         nc.vector.memset(eps_t[:], EPS)
         one_t = const.tile([P, 1], F32, name="one_t")
@@ -129,12 +127,14 @@ def tile_deepseekmultiheadattention_pb_t_kernel(tc, x, wkv_c, kv_a_norm_w, wkv_b
         wk_scales = const.tile([P, H * NOPE], U8, name="wk_scales", align_bytes=64)
 
         def quantise_wkv_c():
-            wc_grouped = const.tile([P, KVR * PACK], BF16, name="wc_grouped", align_bytes=64)
-            nc.vector.tensor_copy(out=wc_grouped[:].rearrange("p (t m j) -> p t m j", t=PACK, j=PACK),
-                                  in_=wc_raw[:].rearrange("p j (m t) -> p t m j", t=PACK))
-            nc.vector.quantize_mx(out=wc_words[:].bitcast(FP8X4), scales=wc_scales[:], in_=wc_grouped[:])
-            nc.vector.tensor_copy(out=gain[:].rearrange("p (t m) -> p t m", t=PACK),
-                                  in_=gain_raw[:].rearrange("p (m t) -> p t m", t=PACK))
+            wc_grouped = const.tile([P, 2, P, 2, PACK], BF16, name="wc_grouped", align_bytes=64)
+            for u in range(2):
+                nc.vector.tensor_copy(out=wc_grouped[:, u, :, :, :],
+                                      in_=wc_raw[:].rearrange("p j (m u e) -> p u m e j", u=2, e=2)[:, u, :, :, :])
+            nc.vector.quantize_mx(out=wc_words[:].bitcast(FP8X4), scales=wc_scales[:],
+                                  in_=wc_grouped[:].rearrange("p u m e j -> p (u m e j)"))
+            nc.vector.tensor_copy(out=gain[:].rearrange("p (u m e) -> p u m e", u=2, e=2),
+                                  in_=gain_raw[:].rearrange("p (m u e) -> p u m e", u=2, e=2))
 
         def quantise_wkv_b():
             by_head = wb_raw[:].rearrange("p t (h d) -> p t h d", h=H)
@@ -230,16 +230,16 @@ def tile_deepseekmultiheadattention_pb_t_kernel(tc, x, wkv_c, kv_a_norm_w, wkv_b
                                            scalar=live["rstd", n][:, a:a + 1], in1=gain[:], op0=ALU.mult, op1=ALU.mult)
 
         def transpose_cn(n):
-            cn = live["cn", n]
-            cnt = psum.tile([P, 2, PACK, P], BF16, name="cnt")
+            cnt = psum.tile([P, 2, 2, P], F32, name="cnt")
             for a in range(2):
-                for t in range(PACK):
-                    nc.tensor.transpose(cnt[:, a, t, :], cn[:, a, P * t:P * t + P], ident_b[:])
+                as_f32 = live["cn", n][:, a, :].bitcast(F32)
+                for u in range(2):
+                    nc.tensor.transpose(cnt[:, a, u, :], as_f32[:, P * u:P * u + P], ident_f[:])
             live["cnt", n] = cnt
 
         def copy_cn(n):
-            dst = grouped(n + 3)[:, PW * PACK:2 * PW * PACK].rearrange("p (a r t) -> p a r t", a=2, t=PACK)
-            src = live["cnt", n][:].rearrange("p a t r -> p a r t")
+            dst = grouped(n + 3)[:, PW * PACK:2 * PW * PACK].bitcast(F32).rearrange("p (a r u) -> p a r u", a=2, u=2)
+            src = live["cnt", n][:].rearrange("p a u r -> p a r u")
             if n >= NPAIR - 2:
                 nc.scalar.copy(out=dst, in_=src)
             else:

@@ -31,6 +31,8 @@ NPAIR = TPP // 2
 PPC = CH // 2
 PW = 2 * P
 RG = 4
+TPARTS = 4
+TROWS = TPP // TPARTS
 X_BUFS = 4
 
 FLOPS = 2 * T * D * KVR + 2 * T * KVR * H * (NOPE + VD)
@@ -74,16 +76,12 @@ def tile_deepseekmultiheadattention_pb_t_kernel(tc, x, wkv_c, kv_a_norm_w, wkv_b
         nc.scalar.dma_start(out=wc_raw[:], in_=wkv_c.rearrange("(p t) f -> p t f", t=PACK))
         nc.scalar.dma_start(out=gain_raw[:], in_=kv_a_norm_w.partition_broadcast(P))
         nc.sync.dma_start(out=wb_raw[:], in_=wkv_b.rearrange("(p t) w -> p t w", t=PACK))
-        load_x(1, [CH])
         nc.sync.dma_start(out=kpe[:], in_=kpe_view)
-        for chunk in range(2, X_BUFS):
+        for chunk in range(1, X_BUFS):
             load_x(chunk, [CH])
 
-        NPOS = NCH + CH
-        pos = const.tile([P, NPOS], F32, name="pos")
-        nc.gpsimd.iota(pos[:, 0:NCH], pattern=[[CH, NCH]], base=0, channel_multiplier=TPP,
-                       allow_small_or_imprecise_dtypes=True)
-        nc.gpsimd.iota(pos[:, NCH:NPOS], pattern=[[1, CH]], base=0, channel_multiplier=0,
+        pos = const.tile([P, TPP], F32, name="pos")
+        nc.gpsimd.iota(pos[:], pattern=[[1, TPP]], base=0, channel_multiplier=TPP,
                        allow_small_or_imprecise_dtypes=True)
         ident_f = const.tile([P, P], F32, name="ident_f")
         make_identity(nc, ident_f[:])
@@ -93,31 +91,46 @@ def tile_deepseekmultiheadattention_pb_t_kernel(tc, x, wkv_c, kv_a_norm_w, wkv_b
         nc.vector.memset(one_t[:], 1.0)
 
         freq = const.tile([P, HALF], F32, name="freq")
-        turns = const.tile([P, NPOS, HALF], F32, name="turns")
-        whole = const.tile([P, NPOS, HALF], I32, name="whole")
-        sin_t = const.tile([P, NPOS, HALF], F32, name="sin_t")
-        cos_t = const.tile([P, NPOS, HALF], F32, name="cos_t")
+        turns = const.tile([P, TPP, HALF], F32, name="turns")
+        whole = const.tile([P, TPP, HALF], I32, name="whole")
+        sin_t = const.tile([P, TPP, HALF], F32, name="sin_t")
+        cos_t = const.tile([P, TPP, HALF], F32, name="cos_t")
         unused = const.tile([P, 1], F32, name="unused")
 
-        def reduce_angles():
-            for j in range(HALF):
-                turns_a_position = 10000.0 ** (-j / float(HALF)) / (2.0 * PI)
-                if j < HALF // 2:
-                    nc.vector.tensor_scalar(out=freq[:, j:j + 1], in0=one_t[:], scalar1=turns_a_position, scalar2=None,
-                                            op0=ALU.mult)
-                else:
-                    nc.scalar.mul(out=freq[:, j:j + 1], in_=one_t[:], mul=turns_a_position)
-            nc.vector.tensor_tensor(out=turns[:], in0=pos[:].unsqueeze(2).to_broadcast([P, NPOS, HALF]),
-                                    in1=freq[:].unsqueeze(1).to_broadcast([P, NPOS, HALF]), op=ALU.mult)
-            nc.vector.tensor_copy(out=whole[:], in_=turns[:])
-            nc.vector.tensor_tensor(out=turns[:], in0=turns[:], in1=whole[:], op=ALU.subtract)
+        def frequencies():
+            for j in range(HALF // 4):
+                nc.vector.tensor_scalar(out=freq[:, j:j + 1], in0=one_t[:],
+                                        scalar1=10000.0 ** (-j / float(HALF)) / (2.0 * PI), scalar2=None, op0=ALU.mult)
+            nc.vector.tensor_scalar(out=freq[:, 8:16], in0=freq[:, 0:8], scalar1=0.1, scalar2=None, op0=ALU.mult)
+            nc.vector.tensor_scalar(out=freq[:, 16:32], in0=freq[:, 0:16], scalar1=0.01, scalar2=None, op0=ALU.mult)
 
-        def make_tables():
-            nc.scalar.activation(out=sin_t[:], in_=turns[:], func=ACT.Sin, scale=2.0 * PI)
-            nc.scalar.activation(out=cos_t[:], in_=turns[:], func=ACT.Sin, scale=PI)
-            nc.scalar.activation(out=unused[:], in_=one_t[:], func=ACT.Abs_reciprocal_sqrt)
-            nc.gpsimd.tensor_tensor(out=cos_t[:], in0=cos_t[:], in1=cos_t[:], op=ALU.mult)
-            nc.gpsimd.tensor_scalar(out=cos_t[:], in0=cos_t[:], scalar1=-2.0, scalar2=1.0, op0=ALU.mult, op1=ALU.add)
+        def table_rows(part):
+            return slice(part * TROWS, (part + 1) * TROWS)
+
+        def angles(part, engine):
+            rows = table_rows(part)
+            shape = [P, TROWS, HALF]
+            engine.tensor_tensor(out=turns[:, rows, :], in0=pos[:, rows].unsqueeze(2).to_broadcast(shape),
+                                 in1=freq[:].unsqueeze(1).to_broadcast(shape), op=ALU.mult)
+
+        def reduce_angles(part):
+            rows = table_rows(part)
+            nc.vector.tensor_copy(out=whole[:, rows, :], in_=turns[:, rows, :])
+            nc.vector.tensor_tensor(out=turns[:, rows, :], in0=turns[:, rows, :], in1=whole[:, rows, :], op=ALU.subtract)
+
+        def load_act_table(func):
+            nc.scalar.activation(out=unused[:], in_=one_t[:], func=func)
+
+        def sines(part):
+            rows = table_rows(part)
+            nc.scalar.activation(out=sin_t[:, rows, :], in_=turns[:, rows, :], func=ACT.Sin, scale=2.0 * PI)
+            nc.scalar.activation(out=cos_t[:, rows, :], in_=turns[:, rows, :], func=ACT.Sin, scale=PI)
+
+        def cosines(part):
+            rows = table_rows(part)
+            nc.gpsimd.tensor_tensor(out=cos_t[:, rows, :], in0=cos_t[:, rows, :], in1=cos_t[:, rows, :], op=ALU.mult)
+            nc.gpsimd.tensor_scalar(out=cos_t[:, rows, :], in0=cos_t[:, rows, :], scalar1=-2.0, scalar2=1.0,
+                                    op0=ALU.mult, op1=ALU.add)
 
         wc_words = const.tile([P, KVR], U32, name="wc_words", align_bytes=64)
         wc_scales = const.tile([P, KVR], U8, name="wc_scales", align_bytes=64)
@@ -151,27 +164,22 @@ def tile_deepseekmultiheadattention_pb_t_kernel(tc, x, wkv_c, kv_a_norm_w, wkv_b
         for chunk in range(NCH):
             ks_chunks[chunk] = const.tile([P, H, CH, NOPE + ROPE], F32, name="ks%d" % chunk)
 
-        def rotate(out_lo, out_hi, src, cos_a, sin_a):
-            by_cos = turn.tile([P, RG, 2, HALF], F32, name="by_cos")
-            by_sin = turn.tile([P, RG, 2, HALF], F32, name="by_sin")
-            nc.gpsimd.tensor_tensor(out=by_cos[:], in0=src, in1=cos_a, op=ALU.mult)
-            nc.gpsimd.tensor_tensor(out=by_sin[:], in0=src, in1=sin_a, op=ALU.mult)
-            nc.gpsimd.tensor_tensor(out=out_lo, in0=by_cos[:, :, 0, :], in1=by_sin[:, :, 1, :], op=ALU.subtract)
-            nc.gpsimd.tensor_tensor(out=out_hi, in0=by_sin[:, :, 0, :], in1=by_cos[:, :, 1, :], op=ALU.add)
-
         def rotate_keys(g):
             shape = [P, RG, 2, HALF]
-            chunk = g * RG // CH
+            tokens = slice(g * RG, (g + 1) * RG)
+            key = kpe[:, tokens, :].rearrange("p i (s j) -> p i s j", s=2)
+            by_cos = turn.tile(shape, F32, name="by_cos")
+            by_sin = turn.tile(shape, F32, name="by_sin")
+            nc.gpsimd.tensor_tensor(out=by_cos[:], in0=key, in1=cos_t[:, tokens, :].unsqueeze(2).to_broadcast(shape),
+                                    op=ALU.mult)
+            nc.gpsimd.tensor_tensor(out=by_sin[:], in0=key, in1=sin_t[:, tokens, :].unsqueeze(2).to_broadcast(shape),
+                                    op=ALU.mult)
             b = g * RG % CH
-            once = turn.tile([P, RG, 2, HALF], F32, name="once")
-            rotate(once[:, :, 0, :], once[:, :, 1, :],
-                   kpe[:, g * RG:(g + 1) * RG, :].rearrange("p i (s j) -> p i s j", s=2),
-                   cos_t[:, NCH + b:NCH + b + RG, :].unsqueeze(2).to_broadcast(shape),
-                   sin_t[:, NCH + b:NCH + b + RG, :].unsqueeze(2).to_broadcast(shape))
-            rows = ks_chunks[chunk][:, 0, b:b + RG, :]
-            rotate(rows[:, :, NOPE:NOPE + HALF], rows[:, :, NOPE + HALF:NOPE + ROPE], once[:],
-                   cos_t[:, chunk:chunk + 1, :].unsqueeze(2).to_broadcast(shape),
-                   sin_t[:, chunk:chunk + 1, :].unsqueeze(2).to_broadcast(shape))
+            rows = ks_chunks[g * RG // CH][:, 0, b:b + RG, :]
+            nc.gpsimd.tensor_tensor(out=rows[:, :, NOPE:NOPE + HALF], in0=by_cos[:, :, 0, :], in1=by_sin[:, :, 1, :],
+                                    op=ALU.subtract)
+            nc.gpsimd.tensor_tensor(out=rows[:, :, NOPE + HALF:NOPE + ROPE], in0=by_sin[:, :, 0, :],
+                                    in1=by_cos[:, :, 1, :], op=ALU.add)
 
         live = {}
 
@@ -285,7 +293,14 @@ def tile_deepseekmultiheadattention_pb_t_kernel(tc, x, wkv_c, kv_a_norm_w, wkv_b
             elif n % PPC == PPC - 1:
                 store(chunk, 0, CH)
 
-        reduce_angles()
+        load_act_table(ACT.Sin)
+        frequencies()
+        angles(0, nc.vector)
+        for part in range(1, TPARTS):
+            angles(part, nc.gpsimd)
+        reduce_angles(0)
+        sines(0)
+        reduce_angles(1)
         quantise_wkv_c()
         for m in range(-1, NPAIR + 4):
             if on(m - 1):
@@ -313,7 +328,15 @@ def tile_deepseekmultiheadattention_pb_t_kernel(tc, x, wkv_c, kv_a_norm_w, wkv_b
             if on(m) or on(m - 3):
                 quantise(m)
             if m == -1:
-                make_tables()
+                sines(1)
+                cosines(0)
+                cosines(1)
+            if m == 0:
+                for part in range(2, TPARTS):
+                    reduce_angles(part)
+                    sines(part)
+                    cosines(part)
+                load_act_table(ACT.Abs_reciprocal_sqrt)
             if m == 1:
                 quantise_wkv_b()
             if 0 <= m < TPP // RG:

@@ -286,8 +286,8 @@ def tile_deepseekmultiheadattention_pb_t_kernel(tc, x, wkv_c, kv_a_norm_w, wkv_b
                 v_chunks[chunk] = vout.tile([P, H, CH, VD], F32, name="v_sb")
             nc.scalar.copy(out=v_chunks[chunk][:, :, i0:i0 + 2, :],
                            in_=live["v", n][:].rearrange("p a (h d) -> p h a d", h=H))
-            nc.scalar.copy(out=ks_chunks[chunk][:, :, i0:i0 + 2, 0:NOPE],
-                           in_=live["k", n][:].rearrange("p a (h d) -> p h a d", h=H))
+            nc.vector.tensor_copy(out=ks_chunks[chunk][:, :, i0:i0 + 2, 0:NOPE],
+                                  in_=live["k", n][:].rearrange("p a (h d) -> p h a d", h=H))
             if chunk == NCH - 1:
                 store(chunk, i0, 2)
             elif n % PPC == PPC - 1:
@@ -309,14 +309,14 @@ def tile_deepseekmultiheadattention_pb_t_kernel(tc, x, wkv_c, kv_a_norm_w, wkv_b
                 matmul_2(m - 4)
             if on(m - 1):
                 statistics(m - 1)
-            if on(m - 4):
-                copy_kv(m - 4)
             if on(m - 2):
                 normalise(m - 2, 0)
             if on(m - 3):
                 copy_cn(m - 3)
             if on(m - 2):
                 normalise(m - 2, 1)
+            if on(m - 4):
+                copy_kv(m - 4)
             if on(m + 1):
                 transpose_x(m + 1)
                 if (m + 1) % PPC == PPC - 1 and (m + 1) // PPC + X_BUFS < NCH:

@@ -239,8 +239,11 @@ def tile_deepseekmultiheadattention_pb_t_kernel(tc, x, wkv_c, kv_a_norm_w, wkv_b
 
         def transpose_cn(n):
             cnt = psum.tile([P, 2, 2, P], F32, name="cnt")
+            cn = live["cn", n]
+            nc.tensor.matmul(cnt[:].rearrange("p a u r -> p (a u r)"), lhsT=cn[:, 0, 0:P], rhs=cn[:, 0, :],
+                             start=True, stop=True)
             for a in range(2):
-                as_f32 = live["cn", n][:, a, :].bitcast(F32)
+                as_f32 = cn[:, a, :].bitcast(F32)
                 for u in range(2):
                     nc.tensor.transpose(cnt[:, a, u, :], as_f32[:, P * u:P * u + P], ident_f[:])
             live["cnt", n] = cnt

@@ -175,11 +175,14 @@ def tile_deepseekmultiheadattention_pb_t_kernel(tc, x, wkv_c, kv_a_norm_w, wkv_b
             nc.gpsimd.tensor_tensor(out=by_sin[:], in0=key, in1=sin_t[:, tokens, :].unsqueeze(2).to_broadcast(shape),
                                     op=ALU.mult)
             b = g * RG % CH
-            rows = ks_chunks[g * RG // CH][:, 0, b:b + RG, :]
-            nc.gpsimd.tensor_tensor(out=rows[:, :, NOPE:NOPE + HALF], in0=by_cos[:, :, 0, :], in1=by_sin[:, :, 1, :],
-                                    op=ALU.subtract)
-            nc.gpsimd.tensor_tensor(out=rows[:, :, NOPE + HALF:NOPE + ROPE], in0=by_sin[:, :, 0, :],
-                                    in1=by_cos[:, :, 1, :], op=ALU.add)
+            both = [P, H, RG, HALF]
+            rows = ks_chunks[g * RG // CH][:, :, b:b + RG, :]
+            nc.gpsimd.tensor_tensor(out=rows[:, :, :, NOPE:NOPE + HALF],
+                                    in0=by_cos[:, :, 0, :].unsqueeze(1).to_broadcast(both),
+                                    in1=by_sin[:, :, 1, :].unsqueeze(1).to_broadcast(both), op=ALU.subtract)
+            nc.gpsimd.tensor_tensor(out=rows[:, :, :, NOPE + HALF:NOPE + ROPE],
+                                    in0=by_sin[:, :, 0, :].unsqueeze(1).to_broadcast(both),
+                                    in1=by_cos[:, :, 1, :].unsqueeze(1).to_broadcast(both), op=ALU.add)
 
         live = {}
 
@@ -276,11 +279,8 @@ def tile_deepseekmultiheadattention_pb_t_kernel(tc, x, wkv_c, kv_a_norm_w, wkv_b
         def store(chunk, i0, count):
             lo = chunk * CH + i0
             hi = lo + count
-            ks = ks_chunks[chunk]
             nc.sync.dma_start(out=v_view[:, :, lo:hi, :], in_=v_chunks[chunk][:, :, i0:i0 + count, :])
-            nc.sync.dma_start(out=ks_view[:, 0, lo:hi, :], in_=ks[:, 0, i0:i0 + count, :])
-            nc.sync.dma_start(out=ks_view[:, 1, lo:hi, 0:NOPE], in_=ks[:, 1, i0:i0 + count, 0:NOPE])
-            nc.sync.dma_start(out=ks_view[:, 1, lo:hi, NOPE:NOPE + ROPE], in_=ks[:, 0, i0:i0 + count, NOPE:NOPE + ROPE])
+            nc.sync.dma_start(out=ks_view[:, :, lo:hi, :], in_=ks_chunks[chunk][:, :, i0:i0 + count, :])
 
         def copy_kv(n):
             chunk = n // PPC

@@ -30,7 +30,8 @@ NCH = TPP // CH
 NPAIR = TPP // 2
 PPC = CH // 2
 PW = 2 * P
-RG = 4
+RG = 2
+SIN_PAIRS = 2
 TPARTS = 4
 TROWS = TPP // TPARTS
 X_BUFS = 4
@@ -57,36 +58,39 @@ def tile_deepseekmultiheadattention_pb_t_kernel(tc, x, wkv_c, kv_a_norm_w, wkv_b
 
         x_chunks = {}
 
-        def load_x(chunk, pieces):
-            xc = xin.tile([P, CH, D], BF16, name="xc")
-            lo = 0
-            for count in pieces:
-                nc.sync.dma_start(out=xc[:, lo:lo + count, :],
-                                  in_=x_view[:, chunk * CH + lo:chunk * CH + lo + count, :])
-                lo += count
-            x_chunks[chunk] = xc
+        def load_x(chunk, lo, count):
+            if lo == 0:
+                x_chunks[chunk] = xin.tile([P, CH, D], BF16, name="xc")
+            nc.sync.dma_start(out=x_chunks[chunk][:, lo:lo + count, :],
+                              in_=x_view[:, chunk * CH + lo:chunk * CH + lo + count, :])
 
         wc_raw = const.tile([P, PACK, KVR], BF16, name="wc_raw")
         wb_raw = const.tile([P, PACK, H * (NOPE + VD)], BF16, name="wb_raw")
-        gain_raw = const.tile([P, KVR], BF16, name="gain_raw")
+        gain_row = const.tile([P, KVR], BF16, name="gain_row")
         gain = const.tile([P, KVR], BF16, name="gain")
         kpe = const.tile([P, TPP, ROPE], BF16, name="kpe")
 
-        load_x(0, [2, CH - 2])
-        nc.scalar.dma_start(out=wc_raw[:], in_=wkv_c.rearrange("(p t) f -> p t f", t=PACK))
-        nc.scalar.dma_start(out=gain_raw[:], in_=kv_a_norm_w.partition_broadcast(P))
+        nc.vector.memset(gain_row[:], 0.0)
+        load_x(0, 0, 2)
+        nc.sync.dma_start(out=wc_raw[:], in_=wkv_c.rearrange("(p t) f -> p t f", t=PACK))
+        nc.sync.dma_start(out=gain_row[0:1, :], in_=kv_a_norm_w.unsqueeze(0))
+        load_x(0, 2, CH - 2)
         nc.sync.dma_start(out=wb_raw[:], in_=wkv_b.rearrange("(p t) w -> p t w", t=PACK))
         nc.sync.dma_start(out=kpe[:], in_=kpe_view)
         for chunk in range(1, X_BUFS):
-            load_x(chunk, [CH])
+            load_x(chunk, 0, CH)
 
         pos = const.tile([P, TPP], F32, name="pos")
         nc.gpsimd.iota(pos[:], pattern=[[1, TPP]], base=0, channel_multiplier=TPP,
                        allow_small_or_imprecise_dtypes=True)
         ident_f = const.tile([P, P], F32, name="ident_f")
         make_identity(nc, ident_f[:])
+        ones = const.tile([P, P], BF16, name="ones")
+        nc.gpsimd.memset(ones[:], 1.0)
         eps_t = const.tile([P, 1], F32, name="eps_t")
         nc.vector.memset(eps_t[:], EPS)
+        minus_half = const.tile([P, 2], F32, name="minus_half")
+        nc.vector.memset(minus_half[:], -0.5)
         one_t = const.tile([P, 1], F32, name="one_t")
         nc.vector.memset(one_t[:], 1.0)
 
@@ -96,6 +100,7 @@ def tile_deepseekmultiheadattention_pb_t_kernel(tc, x, wkv_c, kv_a_norm_w, wkv_b
         sin_t = const.tile([P, TPP, HALF], F32, name="sin_t")
         cos_t = const.tile([P, TPP, HALF], F32, name="cos_t")
         unused = const.tile([P, 1], F32, name="unused")
+        after = const.tile([P, 1], U32, name="after")
 
         def frequencies():
             for j in range(HALF // 4):
@@ -146,8 +151,12 @@ def tile_deepseekmultiheadattention_pb_t_kernel(tc, x, wkv_c, kv_a_norm_w, wkv_b
                                       in_=wc_raw[:].rearrange("p j (m u e) -> p u m e j", u=2, e=2)[:, u, :, :, :])
             nc.vector.quantize_mx(out=wc_words[:].bitcast(FP8X4), scales=wc_scales[:],
                                   in_=wc_grouped[:].rearrange("p u m e j -> p (u m e j)"))
-            nc.vector.tensor_copy(out=gain[:].rearrange("p (u m e) -> p u m e", u=2, e=2),
-                                  in_=gain_raw[:].rearrange("p (m u e) -> p u m e", u=2, e=2))
+
+        def spread_gain():
+            spread = psum.tile([P, KVR], F32, name="c_ps", bufs=4)
+            nc.tensor.matmul(spread[:], lhsT=ones[:], rhs=gain_row[:], start=True, stop=True)
+            nc.scalar.copy(out=gain[:].rearrange("p (u m e) -> p u m e", u=2, e=2),
+                           in_=spread[:].rearrange("p (m u e) -> p u m e", u=2, e=2))
 
         def quantise_wkv_b():
             by_head = wb_raw[:].rearrange("p t (h d) -> p t h d", h=H)
@@ -207,14 +216,13 @@ def tile_deepseekmultiheadattention_pb_t_kernel(tc, x, wkv_c, kv_a_norm_w, wkv_b
             nc.scalar.copy(out=grouped(n)[:, 0:PW * PACK].bitcast(F32).rearrange("p (a r u) -> p a r u", a=2, u=2),
                            in_=live["xt", n][:].rearrange("p a u r -> p a r u"))
 
-        def quantise(period):
-            lo = 0 if on(period) else PW
-            hi = 2 * PW if on(period - 3) else PW
-            words = work.tile([P, 2 * PW], U32, name="words", align_bytes=64)
-            scales = work.tile([P, 2 * PW], U8, name="scales", align_bytes=64)
+        def quantise(period, lo, hi):
+            if ("quantised", period) not in live:
+                live["quantised", period] = (work.tile([P, 2 * PW], U32, name="words", align_bytes=64, bufs=4),
+                                             work.tile([P, 2 * PW], U8, name="scales", align_bytes=64, bufs=4))
+            words, scales = live["quantised", period]
             nc.vector.quantize_mx(out=words[:, lo:hi].bitcast(FP8X4), scales=scales[:, lo:hi],
                                   in_=grouped(period)[:, PACK * lo:PACK * hi])
-            live["quantised", period] = (words, scales)
 
         def matmul_1(n):
             words, scales = live["quantised", n]
@@ -230,9 +238,17 @@ def tile_deepseekmultiheadattention_pb_t_kernel(tc, x, wkv_c, kv_a_norm_w, wkv_b
             for a in range(2):
                 squares = work.tile([P, KVR], BF16, name="squares")
                 nc.scalar.activation(out=squares[:], in_=live["c", n, a][:], func=ACT.Square, accum_out=sums[:, a:a + 1])
-            rstd = small.tile([P, 2], F32, name="rstd")
-            nc.scalar.activation(out=rstd[:], in_=sums[:], func=ACT.Abs_reciprocal_sqrt, scale=1.0 / KVR, bias=eps_t[:])
-            live["rstd", n] = rstd
+            live["sums", n] = sums
+            live["rstd", n] = small.tile([P, 2], F32, name="rstd")
+            if n < SIN_PAIRS:
+                mean = small.tile([P, 2], F32, name="mean")
+                nc.gpsimd.tensor_scalar(out=mean[:], in0=sums[:], scalar1=1.0 / KVR, scalar2=EPS, op0=ALU.mult, op1=ALU.add)
+                nc.gpsimd.tensor_tensor(out=live["rstd", n][:], in0=mean[:], in1=minus_half[:], op=ALU.pow)
+
+        def reciprocal_rms(n, a):
+            if n >= SIN_PAIRS:
+                nc.scalar.activation(out=live["rstd", n][:, a:a + 1], in_=live["sums", n][:, a:a + 1],
+                                     func=ACT.Abs_reciprocal_sqrt, scale=1.0 / KVR, bias=eps_t[:])
 
         def normalise(n, a):
             if a == 0:
@@ -240,39 +256,35 @@ def tile_deepseekmultiheadattention_pb_t_kernel(tc, x, wkv_c, kv_a_norm_w, wkv_b
             nc.vector.scalar_tensor_tensor(out=live["cn", n][:, a, :], in0=live["c", n, a][:],
                                            scalar=live["rstd", n][:, a:a + 1], in1=gain[:], op0=ALU.mult, op1=ALU.mult)
 
-        def transpose_cn(n):
-            cnt = psum.tile([P, 2, 2, P], F32, name="cnt")
-            cn = live["cn", n]
-            nc.tensor.matmul(cnt[:].rearrange("p a u r -> p (a u r)"), lhsT=cn[:, 0, 0:P], rhs=cn[:, 0, :],
-                             start=True, stop=True)
-            for a in range(2):
-                as_f32 = cn[:, a, :].bitcast(F32)
+        def transpose_cn(n, tiles, bank):
+            cnt = psum.tile([P, 2, 2, P], F32, name=bank)
+            for a in tiles:
+                as_f32 = live["cn", n][:, a, :].bitcast(F32)
                 for u in range(2):
                     nc.tensor.transpose(cnt[:, a, u, :], as_f32[:, P * u:P * u + P], ident_f[:])
-            live["cnt", n] = cnt
+                live["cnt", n, a] = cnt
 
-        def copy_cn(n):
-            dst = grouped(n + 3)[:, PW * PACK:2 * PW * PACK].bitcast(F32).rearrange("p (a r u) -> p a r u", a=2, u=2)
-            src = live["cnt", n][:].rearrange("p a u r -> p a r u")
-            if n >= NPAIR - 2:
-                nc.scalar.copy(out=dst, in_=src)
-            else:
-                nc.vector.tensor_copy(out=dst, in_=src)
+        def copy_cn(n, tiles, copy):
+            lo, count = tiles[0], len(tiles)
+            first = (PW + P * lo) * PACK
+            copy(out=grouped(n + 4)[:, first:first + P * count * PACK].bitcast(F32).rearrange("p (a r u) -> p a r u",
+                                                                                              a=count, u=2),
+                 in_=live["cnt", n, lo][:, lo:lo + count, :, :].rearrange("p a u r -> p a r u"))
 
-        def matmul_2(n):
-            words, scales = live["quantised", n + 3]
-            v_ps = psum.tile([P, 2, H * VD], F32, name="v_ps")
-            k_ps = psum.tile([P, 2, H * NOPE], F32, name="k_ps")
-            for a in range(2):
+        def matmul_2(n, tiles, v_bank, k_bank, bufs):
+            words, scales = live["quantised", n + 4]
+            v_ps = psum.tile([P, 2, H * VD], F32, name=v_bank, bufs=bufs)
+            k_ps = psum.tile([P, 2, H * VD], F32, name=k_bank, bufs=bufs)
+            for a in tiles:
                 lo = PW + P * a
                 nc.tensor.matmul_mx(out=v_ps[:, a, :], lhsT=words[:, lo:lo + P].bitcast(FP8X4),
                                     lhsT_scale=scales[:, lo:lo + P],
                                     rhs=wv_words[:].bitcast(FP8X4), rhs_scale=wv_scales[:], start=True, stop=True)
-                nc.tensor.matmul_mx(out=k_ps[:, a, :], lhsT=words[:, lo:lo + P].bitcast(FP8X4),
+                nc.tensor.matmul_mx(out=k_ps[:, a, 0:H * NOPE], lhsT=words[:, lo:lo + P].bitcast(FP8X4),
                                     lhsT_scale=scales[:, lo:lo + P],
                                     rhs=wk_words[:].bitcast(FP8X4), rhs_scale=wk_scales[:], start=True, stop=True)
-            live["v", n] = v_ps
-            live["k", n] = k_ps
+                live["v", n, a] = v_ps
+                live["k", n, a] = k_ps
 
         v_chunks = {}
 
@@ -282,17 +294,18 @@ def tile_deepseekmultiheadattention_pb_t_kernel(tc, x, wkv_c, kv_a_norm_w, wkv_b
             nc.sync.dma_start(out=v_view[:, :, lo:hi, :], in_=v_chunks[chunk][:, :, i0:i0 + count, :])
             nc.sync.dma_start(out=ks_view[:, :, lo:hi, :], in_=ks_chunks[chunk][:, :, i0:i0 + count, :])
 
-        def copy_kv(n):
+        def copy_kv(n, tiles):
             chunk = n // PPC
-            i0 = 2 * (n % PPC)
-            if n % PPC == 0:
+            lo, count = tiles[0], len(tiles)
+            i0 = 2 * (n % PPC) + lo
+            if i0 == 0:
                 v_chunks[chunk] = vout.tile([P, H, CH, VD], F32, name="v_sb")
-            nc.scalar.copy(out=v_chunks[chunk][:, :, i0:i0 + 2, :],
-                           in_=live["v", n][:].rearrange("p a (h d) -> p h a d", h=H))
-            nc.vector.tensor_copy(out=ks_chunks[chunk][:, :, i0:i0 + 2, 0:NOPE],
-                                  in_=live["k", n][:].rearrange("p a (h d) -> p h a d", h=H))
-            if chunk == NCH - 1:
-                store(chunk, i0, 2)
+            nc.scalar.copy(out=v_chunks[chunk][:, :, i0:i0 + count, :],
+                           in_=live["v", n, lo][:, lo:lo + count, :].rearrange("p a (h d) -> p h a d", h=H))
+            nc.vector.tensor_copy(out=ks_chunks[chunk][:, :, i0:i0 + count, 0:NOPE],
+                                  in_=live["k", n, lo][:, lo:lo + count, 0:H * NOPE].rearrange("p a (h d) -> p h a d", h=H))
+            if chunk >= NCH - 2:
+                store(chunk, i0, count)
             elif n % PPC == PPC - 1:
                 store(chunk, 0, CH)
 
@@ -305,42 +318,71 @@ def tile_deepseekmultiheadattention_pb_t_kernel(tc, x, wkv_c, kv_a_norm_w, wkv_b
         sines(0)
         reduce_angles(1)
         quantise_wkv_c()
-        for m in range(-1, NPAIR + 4):
-            if on(m - 1):
-                matmul_1(m - 1)
-            if on(m - 4):
-                matmul_2(m - 4)
-            if on(m - 1):
-                statistics(m - 1)
+        both = (0, 1)
+        for m in range(-1, NPAIR + 2):
             if on(m - 2):
-                normalise(m - 2, 0)
+                matmul_1(m - 2)
+            if on(m - 5):
+                matmul_2(m - 5, both, "v_ps", "k_ps", 1)
+            if on(m - 2):
+                statistics(m - 2)
+                reciprocal_rms(m - 2, 0)
             if on(m - 3):
-                copy_cn(m - 3)
-            if on(m - 2):
-                normalise(m - 2, 1)
+                normalise(m - 3, 0)
             if on(m - 4):
-                copy_kv(m - 4)
+                copy_cn(m - 4, both, nc.vector.tensor_copy)
+            if on(m - 3):
+                normalise(m - 3, 1)
+            if on(m - 5):
+                copy_kv(m - 5, both)
+            if on(m - 2):
+                reciprocal_rms(m - 2, 1)
             if on(m + 1):
                 transpose_x(m + 1)
                 if (m + 1) % PPC == PPC - 1 and (m + 1) // PPC + X_BUFS < NCH:
-                    load_x((m + 1) // PPC + X_BUFS, [CH])
-            if on(m - 2):
-                transpose_cn(m - 2)
+                    load_x((m + 1) // PPC + X_BUFS, 0, CH)
+            if on(m - 3):
+                transpose_cn(m - 3, both, "cnt")
             if on(m + 1):
                 copy_x(m + 1)
-            if on(m) or on(m - 3):
-                quantise(m)
+            if m >= 0:
+                quantise(m, 0 if on(m) else PW, 2 * PW if on(m - 4) else PW)
             if m == -1:
                 sines(1)
                 cosines(0)
                 cosines(1)
             if m == 0:
-                for part in range(2, TPARTS):
-                    reduce_angles(part)
-                    sines(part)
-                    cosines(part)
-                load_act_table(ACT.Abs_reciprocal_sqrt)
+                spread_gain()
+                reduce_angles(2)
             if m == 1:
+                reduce_angles(3)
                 quantise_wkv_b()
-            if 0 <= m < TPP // RG:
-                rotate_keys(m)
+            if 2 <= m < TPARTS:
+                sines(m)
+            if m == 1 + SIN_PAIRS:
+                load_act_table(ACT.Abs_reciprocal_sqrt)
+            if m >= 3:
+                column = 0 if on(m) else PW
+                nc.gpsimd.tensor_copy(out=after[:], in_=live["quantised", m][0][:, column:column + 1])
+                for n in range(m - 3 if m <= NPAIR // 2 else m - 2, m - 2 if m < NPAIR // 2 else m - 1):
+                    rotate_keys(n)
+            if 4 <= m < 2 + TPARTS:
+                cosines(m - 2)
+        last = NPAIR - 1
+        matmul_2(last - 2, both, "v_ps", "k_ps", 1)
+        copy_cn(last - 1, both, nc.scalar.copy)
+        normalise(last, 0)
+        transpose_cn(last, (0,), "xt")
+        normalise(last, 1)
+        transpose_cn(last, (1,), "cnt")
+        copy_kv(last - 2, both)
+        quantise(last + 3, PW, 2 * PW)
+        matmul_2(last - 1, both, "v_ps", "k_ps", 1)
+        copy_cn(last, (0,), nc.scalar.copy)
+        copy_cn(last, (1,), nc.vector.tensor_copy)
+        for a in range(2):
+            quantise(last + 4, PW + P * a, PW + P * a + P)
+        copy_kv(last - 1, both)
+        for a in range(2):
+            matmul_2(last, (a,), "c_ps", "c_ps", 4)
+            copy_kv(last, (a,))

@@ -30,10 +30,14 @@ NCH = TPP // CH
 NPAIR = TPP // 2
 PPC = CH // 2
 PW = 2 * P
+BOTH_HEADS = 2 * CH
 RG = 2
-SIN_PAIRS = 2
+SIN_PAIRS = 3
+EARLY = 2
 TPARTS = 4
 TROWS = TPP // TPARTS
+SINE_PERIODS = [-1, 1, 2, 4]
+COSINE_PERIODS = [1, 2, 4, 8]
 X_BUFS = 4
 
 FLOPS = 2 * T * D * KVR + 2 * T * KVR * H * (NOPE + VD)
@@ -70,7 +74,7 @@ def tile_deepseekmultiheadattention_pb_t_kernel(tc, x, wkv_c, kv_a_norm_w, wkv_b
         gain = const.tile([P, KVR], BF16, name="gain")
         kpe = const.tile([P, TPP, ROPE], BF16, name="kpe")
 
-        nc.vector.memset(gain_row[:], 0.0)
+        nc.gpsimd.memset(gain_row[:], 0.0)
         load_x(0, 0, 2)
         nc.sync.dma_start(out=wc_raw[:], in_=wkv_c.rearrange("(p t) f -> p t f", t=PACK))
         nc.sync.dma_start(out=gain_row[0:1, :], in_=kv_a_norm_w.unsqueeze(0))
@@ -112,14 +116,11 @@ def tile_deepseekmultiheadattention_pb_t_kernel(tc, x, wkv_c, kv_a_norm_w, wkv_b
         def table_rows(part):
             return slice(part * TROWS, (part + 1) * TROWS)
 
-        def angles(part, engine):
-            rows = table_rows(part)
-            shape = [P, TROWS, HALF]
-            engine.tensor_tensor(out=turns[:, rows, :], in0=pos[:, rows].unsqueeze(2).to_broadcast(shape),
-                                 in1=freq[:].unsqueeze(1).to_broadcast(shape), op=ALU.mult)
-
         def reduce_angles(part):
             rows = table_rows(part)
+            shape = [P, TROWS, HALF]
+            nc.vector.tensor_tensor(out=turns[:, rows, :], in0=pos[:, rows].unsqueeze(2).to_broadcast(shape),
+                                    in1=freq[:].unsqueeze(1).to_broadcast(shape), op=ALU.mult)
             nc.vector.tensor_copy(out=whole[:, rows, :], in_=turns[:, rows, :])
             nc.vector.tensor_tensor(out=turns[:, rows, :], in0=turns[:, rows, :], in1=whole[:, rows, :], op=ALU.subtract)
 
@@ -153,10 +154,11 @@ def tile_deepseekmultiheadattention_pb_t_kernel(tc, x, wkv_c, kv_a_norm_w, wkv_b
                                   in_=wc_grouped[:].rearrange("p u m e j -> p (u m e j)"))
 
         def spread_gain():
-            spread = psum.tile([P, KVR], F32, name="c_ps", bufs=4)
-            nc.tensor.matmul(spread[:], lhsT=ones[:], rhs=gain_row[:], start=True, stop=True)
+            spread = psum.tile([P, 2, H * VD], F32, name="v_ps", bufs=1)
+            flat = spread[:].rearrange("p a w -> p (a w)")
+            nc.tensor.matmul(flat, lhsT=ones[:], rhs=gain_row[:], start=True, stop=True)
             nc.scalar.copy(out=gain[:].rearrange("p (u m e) -> p u m e", u=2, e=2),
-                           in_=spread[:].rearrange("p (m u e) -> p u m e", u=2, e=2))
+                           in_=flat.rearrange("p (m u e) -> p u m e", u=2, e=2))
 
         def quantise_wkv_b():
             by_head = wb_raw[:].rearrange("p t (h d) -> p t h d", h=H)
@@ -184,8 +186,9 @@ def tile_deepseekmultiheadattention_pb_t_kernel(tc, x, wkv_c, kv_a_norm_w, wkv_b
             nc.gpsimd.tensor_tensor(out=by_sin[:], in0=key, in1=sin_t[:, tokens, :].unsqueeze(2).to_broadcast(shape),
                                     op=ALU.mult)
             b = g * RG % CH
-            both = [P, H, RG, HALF]
-            rows = ks_chunks[g * RG // CH][:, :, b:b + RG, :]
+            heads = H if g * RG >= TPP - BOTH_HEADS else 1
+            both = [P, heads, RG, HALF]
+            rows = ks_chunks[g * RG // CH][:, 0:heads, b:b + RG, :]
             nc.gpsimd.tensor_tensor(out=rows[:, :, :, NOPE:NOPE + HALF],
                                     in0=by_cos[:, :, 0, :].unsqueeze(1).to_broadcast(both),
                                     in1=by_sin[:, :, 1, :].unsqueeze(1).to_broadcast(both), op=ALU.subtract)
@@ -292,7 +295,14 @@ def tile_deepseekmultiheadattention_pb_t_kernel(tc, x, wkv_c, kv_a_norm_w, wkv_b
             lo = chunk * CH + i0
             hi = lo + count
             nc.sync.dma_start(out=v_view[:, :, lo:hi, :], in_=v_chunks[chunk][:, :, i0:i0 + count, :])
-            nc.sync.dma_start(out=ks_view[:, :, lo:hi, :], in_=ks_chunks[chunk][:, :, i0:i0 + count, :])
+            ks = ks_chunks[chunk]
+            if lo >= TPP - BOTH_HEADS:
+                nc.sync.dma_start(out=ks_view[:, :, lo:hi, :], in_=ks[:, :, i0:i0 + count, :])
+            else:
+                nc.sync.dma_start(out=ks_view[:, 0, lo:hi, :], in_=ks[:, 0, i0:i0 + count, :])
+                nc.sync.dma_start(out=ks_view[:, 1, lo:hi, 0:NOPE], in_=ks[:, 1, i0:i0 + count, 0:NOPE])
+                nc.sync.dma_start(out=ks_view[:, 1, lo:hi, NOPE:NOPE + ROPE],
+                                  in_=ks[:, 0, i0:i0 + count, NOPE:NOPE + ROPE])
 
         def copy_kv(n, tiles):
             chunk = n // PPC
@@ -311,22 +321,18 @@ def tile_deepseekmultiheadattention_pb_t_kernel(tc, x, wkv_c, kv_a_norm_w, wkv_b
 
         load_act_table(ACT.Sin)
         frequencies()
-        angles(0, nc.vector)
-        for part in range(1, TPARTS):
-            angles(part, nc.gpsimd)
         reduce_angles(0)
-        sines(0)
-        reduce_angles(1)
         quantise_wkv_c()
         both = (0, 1)
         for m in range(-1, NPAIR + 2):
-            if on(m - 2):
-                matmul_1(m - 2)
+            first = m - 1 if 0 <= m - 1 < EARLY else m - 2 if m - 2 >= EARLY else -1
+            if on(first):
+                matmul_1(first)
             if on(m - 5):
                 matmul_2(m - 5, both, "v_ps", "k_ps", 1)
-            if on(m - 2):
-                statistics(m - 2)
-                reciprocal_rms(m - 2, 0)
+            if on(first):
+                statistics(first)
+                reciprocal_rms(first, 0)
             if on(m - 3):
                 normalise(m - 3, 0)
             if on(m - 4):
@@ -335,8 +341,8 @@ def tile_deepseekmultiheadattention_pb_t_kernel(tc, x, wkv_c, kv_a_norm_w, wkv_b
                 normalise(m - 3, 1)
             if on(m - 5):
                 copy_kv(m - 5, both)
-            if on(m - 2):
-                reciprocal_rms(m - 2, 1)
+            if on(first):
+                reciprocal_rms(first, 1)
             if on(m + 1):
                 transpose_x(m + 1)
                 if (m + 1) % PPC == PPC - 1 and (m + 1) // PPC + X_BUFS < NCH:
@@ -347,27 +353,23 @@ def tile_deepseekmultiheadattention_pb_t_kernel(tc, x, wkv_c, kv_a_norm_w, wkv_b
                 copy_x(m + 1)
             if m >= 0:
                 quantise(m, 0 if on(m) else PW, 2 * PW if on(m - 4) else PW)
-            if m == -1:
-                sines(1)
-                cosines(0)
-                cosines(1)
+            if 0 <= m < TPARTS - 1:
+                reduce_angles(m + 1)
             if m == 0:
                 spread_gain()
-                reduce_angles(2)
-            if m == 1:
-                reduce_angles(3)
-                quantise_wkv_b()
-            if 2 <= m < TPARTS:
-                sines(m)
-            if m == 1 + SIN_PAIRS:
+            if m in SINE_PERIODS:
+                sines(SINE_PERIODS.index(m))
+            if m in COSINE_PERIODS:
+                cosines(COSINE_PERIODS.index(m))
+            if m == SINE_PERIODS[-1]:
                 load_act_table(ACT.Abs_reciprocal_sqrt)
-            if m >= 3:
+            if m == 3:
+                quantise_wkv_b()
+            if m >= 4:
                 column = 0 if on(m) else PW
                 nc.gpsimd.tensor_copy(out=after[:], in_=live["quantised", m][0][:, column:column + 1])
-                for n in range(m - 3 if m <= NPAIR // 2 else m - 2, m - 2 if m < NPAIR // 2 else m - 1):
+                for n in range(m - 4 if m <= NPAIR // 2 else m - 2, m - 3 if m < NPAIR // 2 else m - 1):
                     rotate_keys(n)
-            if 4 <= m < 2 + TPARTS:
-                cosines(m - 2)
         last = NPAIR - 1
         matmul_2(last - 2, both, "v_ps", "k_ps", 1)
         copy_cn(last - 1, both, nc.scalar.copy)

@@ -101,8 +101,9 @@ def tile_deepseekmultiheadattention_pb_t_kernel(tc, x, wkv_c, kv_a_norm_w, wkv_b
         freq = const.tile([P, HALF], F32, name="freq")
         turns = const.tile([P, TPP, HALF], F32, name="turns")
         whole = const.tile([P, TPP, HALF], I32, name="whole")
-        sin_t = const.tile([P, TPP, HALF], F32, name="sin_t")
-        cos_t = const.tile([P, TPP, HALF], F32, name="cos_t")
+        cos_sin = const.tile([P, TPP, 2, HALF], F32, name="cos_sin")
+        cos_t = cos_sin[:, :, 0, :]
+        sin_t = cos_sin[:, :, 1, :]
         unused = const.tile([P, 1], F32, name="unused")
         after = const.tile([P, 1], U32, name="after")
 
@@ -176,25 +177,22 @@ def tile_deepseekmultiheadattention_pb_t_kernel(tc, x, wkv_c, kv_a_norm_w, wkv_b
             ks_chunks[chunk] = const.tile([P, H, CH, NOPE + ROPE], F32, name="ks%d" % chunk)
 
         def rotate_keys(g):
-            shape = [P, RG, 2, HALF]
+            shape = [P, RG, 2, 2, HALF]
             tokens = slice(g * RG, (g + 1) * RG)
-            key = kpe[:, tokens, :].rearrange("p i (s j) -> p i s j", s=2)
-            by_cos = turn.tile(shape, F32, name="by_cos")
-            by_sin = turn.tile(shape, F32, name="by_sin")
-            nc.gpsimd.tensor_tensor(out=by_cos[:], in0=key, in1=cos_t[:, tokens, :].unsqueeze(2).to_broadcast(shape),
-                                    op=ALU.mult)
-            nc.gpsimd.tensor_tensor(out=by_sin[:], in0=key, in1=sin_t[:, tokens, :].unsqueeze(2).to_broadcast(shape),
-                                    op=ALU.mult)
+            by = turn.tile(shape, F32, name="by")
+            nc.gpsimd.tensor_tensor(out=by[:], op=ALU.mult,
+                                    in0=kpe[:, tokens, :].rearrange("p i (s j) -> p i s j", s=2).unsqueeze(2).to_broadcast(shape),
+                                    in1=cos_sin[:, tokens, :, :].unsqueeze(3).to_broadcast(shape))
             b = g * RG % CH
             heads = H if g * RG >= TPP - BOTH_HEADS else 1
             both = [P, heads, RG, HALF]
             rows = ks_chunks[g * RG // CH][:, 0:heads, b:b + RG, :]
             nc.gpsimd.tensor_tensor(out=rows[:, :, :, NOPE:NOPE + HALF],
-                                    in0=by_cos[:, :, 0, :].unsqueeze(1).to_broadcast(both),
-                                    in1=by_sin[:, :, 1, :].unsqueeze(1).to_broadcast(both), op=ALU.subtract)
+                                    in0=by[:, :, 0, 0, :].unsqueeze(1).to_broadcast(both),
+                                    in1=by[:, :, 1, 1, :].unsqueeze(1).to_broadcast(both), op=ALU.subtract)
             nc.gpsimd.tensor_tensor(out=rows[:, :, :, NOPE + HALF:NOPE + ROPE],
-                                    in0=by_sin[:, :, 0, :].unsqueeze(1).to_broadcast(both),
-                                    in1=by_cos[:, :, 1, :].unsqueeze(1).to_broadcast(both), op=ALU.add)
+                                    in0=by[:, :, 1, 0, :].unsqueeze(1).to_broadcast(both),
+                                    in1=by[:, :, 0, 1, :].unsqueeze(1).to_broadcast(both), op=ALU.add)
 
         live = {}
 

from contextlib import ExitStack

import concourse.mybir as mybir
from concourse.masks import make_identity

F32 = mybir.dt.float32
BF16 = mybir.dt.bfloat16
U32 = mybir.dt.uint32
U8 = mybir.dt.uint8
I32 = mybir.dt.int32
FP8X4 = mybir.dt.float8_e4m3fn_x4
ALU = mybir.AluOpType
ACT = mybir.ActivationFunctionType

P = 128
PACK = 4
T = 8192
D = 512
KVR = 512
H = 2
NOPE = 64
VD = 128
ROPE = 64
HALF = ROPE // 2
EPS = 1.1920928955078125e-07
PI = 3.141592653589793
TPP = T // P
CH = 8
NCH = TPP // CH
NPAIR = TPP // 2
PPC = CH // 2
PW = 2 * P
BOTH_HEADS = 2 * CH
RG = 2
SIN_PAIRS = 3
EARLY = 2
TPARTS = 4
TROWS = TPP // TPARTS
SINE_PERIODS = [-1, 1, 2, 4]
COSINE_PERIODS = [1, 2, 4, 8]
X_BUFS = 4

FLOPS = 2 * T * D * KVR + 2 * T * KVR * H * (NOPE + VD)


def tile_deepseekmultiheadattention_pb_t_kernel(tc, x, wkv_c, kv_a_norm_w, wkv_b, k_pe, out_0, out_1):
    nc = tc.nc
    x_view = x.flatten_outer_dims().rearrange("(p i) k -> p i k", i=TPP)
    kpe_view = k_pe.flatten_outer_dims().rearrange("(p i) d -> p i d", i=TPP)
    ks_view = out_0.rearrange("o h (p i) d -> p (o h) i d", i=TPP)
    v_view = out_1.rearrange("o h (p i) d -> p (o h) i d", i=TPP)

    with ExitStack() as ctx:
        const = ctx.enter_context(tc.tile_pool(name="const", bufs=1))
        xin = ctx.enter_context(tc.tile_pool(name="xin", bufs=X_BUFS))
        work = ctx.enter_context(tc.tile_pool(name="work", bufs=3))
        small = ctx.enter_context(tc.tile_pool(name="small", bufs=4))
        vout = ctx.enter_context(tc.tile_pool(name="vout", bufs=3))
        turn = ctx.enter_context(tc.tile_pool(name="turn", bufs=2))
        psum = ctx.enter_context(tc.psum_pool(name="psum", bufs=1))
        ctx.enter_context(tc.manual_schedule())

        x_chunks = {}

        def load_x(chunk, lo, count):
            if lo == 0:
                x_chunks[chunk] = xin.tile([P, CH, D], BF16, name="xc")
            nc.sync.dma_start(out=x_chunks[chunk][:, lo:lo + count, :],
                              in_=x_view[:, chunk * CH + lo:chunk * CH + lo + count, :])

        wc_raw = const.tile([P, PACK, KVR], BF16, name="wc_raw")
        wb_raw = const.tile([P, PACK, H * (NOPE + VD)], BF16, name="wb_raw")
        gain_row = const.tile([P, KVR], BF16, name="gain_row")
        gain = const.tile([P, KVR], BF16, name="gain")
        kpe = const.tile([P, TPP, ROPE], BF16, name="kpe")

        nc.gpsimd.memset(gain_row[:], 0.0)
        load_x(0, 0, 2)
        nc.sync.dma_start(out=wc_raw[:], in_=wkv_c.rearrange("(p t) f -> p t f", t=PACK))
        nc.sync.dma_start(out=gain_row[0:1, :], in_=kv_a_norm_w.unsqueeze(0))
        load_x(0, 2, CH - 2)
        nc.sync.dma_start(out=wb_raw[:], in_=wkv_b.rearrange("(p t) w -> p t w", t=PACK))
        nc.sync.dma_start(out=kpe[:], in_=kpe_view)
        for chunk in range(1, X_BUFS):
            load_x(chunk, 0, CH)

        pos = const.tile([P, TPP], F32, name="pos")
        nc.gpsimd.iota(pos[:], pattern=[[1, TPP]], base=0, channel_multiplier=TPP,
                       allow_small_or_imprecise_dtypes=True)
        ident_f = const.tile([P, P], F32, name="ident_f")
        make_identity(nc, ident_f[:])
        ones = const.tile([P, P], BF16, name="ones")
        nc.gpsimd.memset(ones[:], 1.0)
        eps_t = const.tile([P, 1], F32, name="eps_t")
        nc.vector.memset(eps_t[:], EPS)
        minus_half = const.tile([P, 2], F32, name="minus_half")
        nc.vector.memset(minus_half[:], -0.5)
        one_t = const.tile([P, 1], F32, name="one_t")
        nc.vector.memset(one_t[:], 1.0)

        freq = const.tile([P, HALF], F32, name="freq")
        turns = const.tile([P, TPP, HALF], F32, name="turns")
        whole = const.tile([P, TPP, HALF], I32, name="whole")
        cos_sin = const.tile([P, TPP, 2, HALF], F32, name="cos_sin")
        cos_t = cos_sin[:, :, 0, :]
        sin_t = cos_sin[:, :, 1, :]
        unused = const.tile([P, 1], F32, name="unused")
        after = const.tile([P, 1], U32, name="after")

        def frequencies():
            for j in range(HALF // 4):
                nc.vector.tensor_scalar(out=freq[:, j:j + 1], in0=one_t[:],
                                        scalar1=10000.0 ** (-j / float(HALF)) / (2.0 * PI), scalar2=None, op0=ALU.mult)
            nc.vector.tensor_scalar(out=freq[:, 8:16], in0=freq[:, 0:8], scalar1=0.1, scalar2=None, op0=ALU.mult)
            nc.vector.tensor_scalar(out=freq[:, 16:32], in0=freq[:, 0:16], scalar1=0.01, scalar2=None, op0=ALU.mult)

        def table_rows(part):
            return slice(part * TROWS, (part + 1) * TROWS)

        def reduce_angles(part):
            rows = table_rows(part)
            shape = [P, TROWS, HALF]
            nc.vector.tensor_tensor(out=turns[:, rows, :], in0=pos[:, rows].unsqueeze(2).to_broadcast(shape),
                                    in1=freq[:].unsqueeze(1).to_broadcast(shape), op=ALU.mult)
            nc.vector.tensor_copy(out=whole[:, rows, :], in_=turns[:, rows, :])
            nc.vector.tensor_tensor(out=turns[:, rows, :], in0=turns[:, rows, :], in1=whole[:, rows, :], op=ALU.subtract)

        def load_act_table(func):
            nc.scalar.activation(out=unused[:], in_=one_t[:], func=func)

        def sines(part):
            rows = table_rows(part)
            nc.scalar.activation(out=sin_t[:, rows, :], in_=turns[:, rows, :], func=ACT.Sin, scale=2.0 * PI)
            nc.scalar.activation(out=cos_t[:, rows, :], in_=turns[:, rows, :], func=ACT.Sin, scale=PI)

        def cosines(part):
            rows = table_rows(part)
            nc.gpsimd.tensor_tensor(out=cos_t[:, rows, :], in0=cos_t[:, rows, :], in1=cos_t[:, rows, :], op=ALU.mult)
            nc.gpsimd.tensor_scalar(out=cos_t[:, rows, :], in0=cos_t[:, rows, :], scalar1=-2.0, scalar2=1.0,
                                    op0=ALU.mult, op1=ALU.add)

        wc_words = const.tile([P, KVR], U32, name="wc_words", align_bytes=64)
        wc_scales = const.tile([P, KVR], U8, name="wc_scales", align_bytes=64)
        wv_words = const.tile([P, H * VD], U32, name="wv_words", align_bytes=64)
        wv_scales = const.tile([P, H * VD], U8, name="wv_scales", align_bytes=64)
        wk_words = const.tile([P, H * NOPE], U32, name="wk_words", align_bytes=64)
        wk_scales = const.tile([P, H * NOPE], U8, name="wk_scales", align_bytes=64)

        def quantise_wkv_c():
            wc_grouped = const.tile([P, 2, P, 2, PACK], BF16, name="wc_grouped", align_bytes=64)
            for u in range(2):
                nc.vector.tensor_copy(out=wc_grouped[:, u, :, :, :],
                                      in_=wc_raw[:].rearrange("p j (m u e) -> p u m e j", u=2, e=2)[:, u, :, :, :])
            nc.vector.quantize_mx(out=wc_words[:].bitcast(FP8X4), scales=wc_scales[:],
                                  in_=wc_grouped[:].rearrange("p u m e j -> p (u m e j)"))

        def spread_gain():
            spread = psum.tile([P, 2, H * VD], F32, name="v_ps", bufs=1)
            flat = spread[:].rearrange("p a w -> p (a w)")
            nc.tensor.matmul(flat, lhsT=ones[:], rhs=gain_row[:], start=True, stop=True)
            nc.scalar.copy(out=gain[:].rearrange("p (u m e) -> p u m e", u=2, e=2),
                           in_=flat.rearrange("p (m u e) -> p u m e", u=2, e=2))

        def quantise_wkv_b():
            by_head = wb_raw[:].rearrange("p t (h d) -> p t h d", h=H)
            wv_grouped = const.tile([P, H, VD, PACK], BF16, name="wv_grouped", align_bytes=64)
            wk_grouped = const.tile([P, H, NOPE, PACK], BF16, name="wk_grouped", align_bytes=64)
            nc.vector.tensor_copy(out=wv_grouped[:], in_=by_head[:, :, :, NOPE:NOPE + VD].rearrange("p t h d -> p h d t"))
            nc.vector.tensor_copy(out=wk_grouped[:], in_=by_head[:, :, :, 0:NOPE].rearrange("p t h d -> p h d t"))
            nc.vector.quantize_mx(out=wv_words[:].bitcast(FP8X4), scales=wv_scales[:],
                                  in_=wv_grouped[:].rearrange("p h d t -> p (h d t)"))
            nc.vector.quantize_mx(out=wk_words[:].bitcast(FP8X4), scales=wk_scales[:],
                                  in_=wk_grouped[:].rearrange("p h d t -> p (h d t)"))

        ks_chunks = {}
        for chunk in range(NCH):
            ks_chunks[chunk] = const.tile([P, H, CH, NOPE + ROPE], F32, name="ks%d" % chunk)

        def rotate_keys(g):
            shape = [P, RG, 2, 2, HALF]
            tokens = slice(g * RG, (g + 1) * RG)
            by = turn.tile(shape, F32, name="by")
            nc.gpsimd.tensor_tensor(out=by[:], op=ALU.mult,
                                    in0=kpe[:, tokens, :].rearrange("p i (s j) -> p i s j", s=2).unsqueeze(2).to_broadcast(shape),
                                    in1=cos_sin[:, tokens, :, :].unsqueeze(3).to_broadcast(shape))
            b = g * RG % CH
            heads = H if g * RG >= TPP - BOTH_HEADS else 1
            both = [P, heads, RG, HALF]
            rows = ks_chunks[g * RG // CH][:, 0:heads, b:b + RG, :]
            nc.gpsimd.tensor_tensor(out=rows[:, :, :, NOPE:NOPE + HALF],
                                    in0=by[:, :, 0, 0, :].unsqueeze(1).to_broadcast(both),
                                    in1=by[:, :, 1, 1, :].unsqueeze(1).to_broadcast(both), op=ALU.subtract)
            nc.gpsimd.tensor_tensor(out=rows[:, :, :, NOPE + HALF:NOPE + ROPE],
                                    in0=by[:, :, 1, 0, :].unsqueeze(1).to_broadcast(both),
                                    in1=by[:, :, 0, 1, :].unsqueeze(1).to_broadcast(both), op=ALU.add)

        live = {}

        def on(n):
            return 0 <= n < NPAIR

        def grouped(period):
            if ("grouped", period) not in live:
                live["grouped", period] = work.tile([P, 2 * PW * PACK], BF16, name="grouped", align_bytes=64)
            return live["grouped", period]

        def transpose_x(n):
            xc = x_chunks[n // PPC]
            xt = psum.tile([P, 2, 2, P], F32, name="xt")
            for a in range(2):
                as_f32 = xc[:, 2 * (n % PPC) + a, :].bitcast(F32)
                for u in range(2):
                    nc.tensor.transpose(xt[:, a, u, :], as_f32[:, u:2 * P:2], ident_f[:])
            live["xt", n] = xt

        def copy_x(n):
            nc.scalar.copy(out=grouped(n)[:, 0:PW * PACK].bitcast(F32).rearrange("p (a r u) -> p a r u", a=2, u=2),
                           in_=live["xt", n][:].rearrange("p a u r -> p a r u"))

        def quantise(period, lo, hi):
            if ("quantised", period) not in live:
                live["quantised", period] = (work.tile([P, 2 * PW], U32, name="words", align_bytes=64, bufs=4),
                                             work.tile([P, 2 * PW], U8, name="scales", align_bytes=64, bufs=4))
            words, scales = live["quantised", period]
            nc.vector.quantize_mx(out=words[:, lo:hi].bitcast(FP8X4), scales=scales[:, lo:hi],
                                  in_=grouped(period)[:, PACK * lo:PACK * hi])

        def matmul_1(n):
            words, scales = live["quantised", n]
            for a in range(2):
                c_ps = psum.tile([P, KVR], F32, name="c_ps", bufs=4)
                nc.tensor.matmul_mx(out=c_ps[:], lhsT=words[:, P * a:P * a + P].bitcast(FP8X4),
                                    lhsT_scale=scales[:, P * a:P * a + P],
                                    rhs=wc_words[:].bitcast(FP8X4), rhs_scale=wc_scales[:], start=True, stop=True)
                live["c", n, a] = c_ps

        def statistics(n):
            sums = small.tile([P, 2], F32, name="sums")
            for a in range(2):
                squares = work.tile([P, KVR], BF16, name="squares")
                nc.scalar.activation(out=squares[:], in_=live["c", n, a][:], func=ACT.Square, accum_out=sums[:, a:a + 1])
            live["sums", n] = sums
            live["rstd", n] = small.tile([P, 2], F32, name="rstd")
            if n < SIN_PAIRS:
                mean = small.tile([P, 2], F32, name="mean")
                nc.gpsimd.tensor_scalar(out=mean[:], in0=sums[:], scalar1=1.0 / KVR, scalar2=EPS, op0=ALU.mult, op1=ALU.add)
                nc.gpsimd.tensor_tensor(out=live["rstd", n][:], in0=mean[:], in1=minus_half[:], op=ALU.pow)

        def reciprocal_rms(n, a):
            if n >= SIN_PAIRS:
                nc.scalar.activation(out=live["rstd", n][:, a:a + 1], in_=live["sums", n][:, a:a + 1],
                                     func=ACT.Abs_reciprocal_sqrt, scale=1.0 / KVR, bias=eps_t[:])

        def normalise(n, a):
            if a == 0:
                live["cn", n] = work.tile([P, 2, KVR], BF16, name="cn")
            nc.vector.scalar_tensor_tensor(out=live["cn", n][:, a, :], in0=live["c", n, a][:],
                                           scalar=live["rstd", n][:, a:a + 1], in1=gain[:], op0=ALU.mult, op1=ALU.mult)

        def transpose_cn(n, tiles, bank):
            cnt = psum.tile([P, 2, 2, P], F32, name=bank)
            for a in tiles:
                as_f32 = live["cn", n][:, a, :].bitcast(F32)
                for u in range(2):
                    nc.tensor.transpose(cnt[:, a, u, :], as_f32[:, P * u:P * u + P], ident_f[:])
                live["cnt", n, a] = cnt

        def copy_cn(n, tiles, copy):
            lo, count = tiles[0], len(tiles)
            first = (PW + P * lo) * PACK
            copy(out=grouped(n + 4)[:, first:first + P * count * PACK].bitcast(F32).rearrange("p (a r u) -> p a r u",
                                                                                              a=count, u=2),
                 in_=live["cnt", n, lo][:, lo:lo + count, :, :].rearrange("p a u r -> p a r u"))

        def matmul_2(n, tiles, v_bank, k_bank, bufs):
            words, scales = live["quantised", n + 4]
            v_ps = psum.tile([P, 2, H * VD], F32, name=v_bank, bufs=bufs)
            k_ps = psum.tile([P, 2, H * VD], F32, name=k_bank, bufs=bufs)
            for a in tiles:
                lo = PW + P * a
                nc.tensor.matmul_mx(out=v_ps[:, a, :], lhsT=words[:, lo:lo + P].bitcast(FP8X4),
                                    lhsT_scale=scales[:, lo:lo + P],
                                    rhs=wv_words[:].bitcast(FP8X4), rhs_scale=wv_scales[:], start=True, stop=True)
                nc.tensor.matmul_mx(out=k_ps[:, a, 0:H * NOPE], lhsT=words[:, lo:lo + P].bitcast(FP8X4),
                                    lhsT_scale=scales[:, lo:lo + P],
                                    rhs=wk_words[:].bitcast(FP8X4), rhs_scale=wk_scales[:], start=True, stop=True)
                live["v", n, a] = v_ps
                live["k", n, a] = k_ps

        v_chunks = {}

        def store(chunk, i0, count):
            lo = chunk * CH + i0
            hi = lo + count
            nc.sync.dma_start(out=v_view[:, :, lo:hi, :], in_=v_chunks[chunk][:, :, i0:i0 + count, :])
            ks = ks_chunks[chunk]
            if lo >= TPP - BOTH_HEADS:
                nc.sync.dma_start(out=ks_view[:, :, lo:hi, :], in_=ks[:, :, i0:i0 + count, :])
            else:
                nc.sync.dma_start(out=ks_view[:, 0, lo:hi, :], in_=ks[:, 0, i0:i0 + count, :])
                nc.sync.dma_start(out=ks_view[:, 1, lo:hi, 0:NOPE], in_=ks[:, 1, i0:i0 + count, 0:NOPE])
                nc.sync.dma_start(out=ks_view[:, 1, lo:hi, NOPE:NOPE + ROPE],
                                  in_=ks[:, 0, i0:i0 + count, NOPE:NOPE + ROPE])

        def copy_kv(n, tiles):
            chunk = n // PPC
            lo, count = tiles[0], len(tiles)
            i0 = 2 * (n % PPC) + lo
            if i0 == 0:
                v_chunks[chunk] = vout.tile([P, H, CH, VD], F32, name="v_sb")
            nc.scalar.copy(out=v_chunks[chunk][:, :, i0:i0 + count, :],
                           in_=live["v", n, lo][:, lo:lo + count, :].rearrange("p a (h d) -> p h a d", h=H))
            nc.vector.tensor_copy(out=ks_chunks[chunk][:, :, i0:i0 + count, 0:NOPE],
                                  in_=live["k", n, lo][:, lo:lo + count, 0:H * NOPE].rearrange("p a (h d) -> p h a d", h=H))
            if chunk >= NCH - 2:
                store(chunk, i0, count)
            elif n % PPC == PPC - 1:
                store(chunk, 0, CH)

        load_act_table(ACT.Sin)
        frequencies()
        reduce_angles(0)
        quantise_wkv_c()
        both = (0, 1)
        for m in range(-1, NPAIR + 2):
            first = m - 1 if 0 <= m - 1 < EARLY else m - 2 if m - 2 >= EARLY else -1
            if on(first):
                matmul_1(first)
            if on(m - 5):
                matmul_2(m - 5, both, "v_ps", "k_ps", 1)
            if on(first):
                statistics(first)
                reciprocal_rms(first, 0)
            if on(m - 3):
                normalise(m - 3, 0)
            if on(m - 4):
                copy_cn(m - 4, both, nc.vector.tensor_copy)
            if on(m - 3):
                normalise(m - 3, 1)
            if on(m - 5):
                copy_kv(m - 5, both)
            if on(first):
                reciprocal_rms(first, 1)
            if on(m + 1):
                transpose_x(m + 1)
                if (m + 1) % PPC == PPC - 1 and (m + 1) // PPC + X_BUFS < NCH:
                    load_x((m + 1) // PPC + X_BUFS, 0, CH)
            if on(m - 3):
                transpose_cn(m - 3, both, "cnt")
            if on(m + 1):
                copy_x(m + 1)
            if m >= 0:
                quantise(m, 0 if on(m) else PW, 2 * PW if on(m - 4) else PW)
            if 0 <= m < TPARTS - 1:
                reduce_angles(m + 1)
            if m == 0:
                spread_gain()
            if m in SINE_PERIODS:
                sines(SINE_PERIODS.index(m))
            if m in COSINE_PERIODS:
                cosines(COSINE_PERIODS.index(m))
            if m == SINE_PERIODS[-1]:
                load_act_table(ACT.Abs_reciprocal_sqrt)
            if m == 3:
                quantise_wkv_b()
            if m >= 4:
                column = 0 if on(m) else PW
                nc.gpsimd.tensor_copy(out=after[:], in_=live["quantised", m][0][:, column:column + 1])
                for n in range(m - 4 if m <= NPAIR // 2 else m - 2, m - 3 if m < NPAIR // 2 else m - 1):
                    rotate_keys(n)
        last = NPAIR - 1
        matmul_2(last - 2, both, "v_ps", "k_ps", 1)
        copy_cn(last - 1, both, nc.scalar.copy)
        normalise(last, 0)
        transpose_cn(last, (0,), "xt")
        normalise(last, 1)
        transpose_cn(last, (1,), "cnt")
        copy_kv(last - 2, both)
        quantise(last + 3, PW, 2 * PW)
        matmul_2(last - 1, both, "v_ps", "k_ps", 1)
        copy_cn(last, (0,), nc.scalar.copy)
        copy_cn(last, (1,), nc.vector.tensor_copy)
        for a in range(2):
            quantise(last + 4, PW + P * a, PW + P * a + P)
        copy_kv(last - 1, both)
        for a in range(2):
            matmul_2(last, (a,), "c_ps", "c_ps", 4)
            copy_kv(last, (a,))
